import numpy as np
import ml_dtypes


def mxq(x, axis, fmt="e4m3"):
    dtype, down = {"e4m3": (ml_dtypes.float8_e4m3fn, 7), "e5m2": (ml_dtypes.float8_e5m2, 14)}[fmt]
    v = np.moveaxis(np.asarray(x, np.float32).astype(ml_dtypes.bfloat16).astype(np.float64), axis, -1)
    blocks = v.reshape(v.shape[:-1] + (-1, 32))
    amax = np.abs(blocks).max(-1, keepdims=True)
    byte = np.maximum(np.where(amax > 0, np.frexp(amax)[1] - 1 + 127, 0) - down, 1)
    scale = np.exp2(byte - 127.0)
    codes = (blocks / scale).astype(np.float32).astype(dtype).astype(np.float64)
    return np.moveaxis((codes * scale).reshape(v.shape), -1, axis)


WIDE = False


def mx_kscale(k):
    if not WIDE:
        return np.ones(k)
    levels = np.array([10, -10, 5, -5, 0])
    a = np.random.permutation(np.resize(levels, k // 512 * 4)).reshape(k // 512, 4)
    idx = np.arange(k)
    return np.exp2(a[idx // 512, idx % 128 // 32])


BF16 = ml_dtypes.bfloat16


def bf(x):
    return np.asarray(x, np.float32).astype(BF16)


def f64(x):
    return np.asarray(x).astype(np.float64)


E2M1 = np.array([0.0, 0.5, 1.0, 1.5, 2.0, 3.0, 4.0, 6.0, -0.0, -0.5, -1.0, -1.5, -2.0, -3.0, -4.0, -6.0])


def pack_weight(w, fmt):
    k, n = w.shape
    w = f64(bf(w)).reshape(k // 32, 32, n)
    amax = np.abs(w).max(1)
    if fmt == "e4m3":
        byte = np.frexp(amax)[1] - 1 + 127 - 7
    else:
        mant, ex = np.frexp(amax / 6.0)
        byte = np.where(mant > 0.5, ex, ex - 1) + 127
    byte = np.clip(np.where(amax > 0, byte, 1), 1, 254)
    scaled = (w * np.exp2(127.0 - byte)[:, None, :]).reshape(k, n).astype(np.float32)
    by_word = np.ascontiguousarray(scaled.reshape(k // 512, 128, 4, n).transpose(0, 1, 3, 2))
    if fmt == "e4m3":
        words = by_word.astype(ml_dtypes.float8_e4m3fn).view(np.uint8)
    else:
        c = by_word.astype(ml_dtypes.float4_e2m1fn).view(np.uint8) & 0xF
        words = c[..., 0::2] | (c[..., 1::2] << 4)
    return np.ascontiguousarray(words), np.ascontiguousarray(byte.astype(np.uint8).reshape(k // 512, 16, n))


def unpack_weight(words, scales, fmt):
    g, p, n, _ = words.shape
    if fmt == "e4m3":
        vals = np.ascontiguousarray(words).view(ml_dtypes.float8_e4m3fn).astype(np.float64)
    else:
        nib = np.empty((g, p, n, 4), np.uint8)
        nib[..., 0::2] = words & 0xF
        nib[..., 1::2] = words >> 4
        vals = E2M1[nib]
    vals = vals * np.repeat(np.exp2(scales.astype(np.float64) - 127.0), 8, axis=1)[..., None]
    return vals.transpose(0, 1, 3, 2).reshape(g * 512, n)

def pack4(w):
    words, scales = pack_weight(w, "e2m1")
    return words.reshape(words.shape[0], 128, -1), scales


def unpack4(words, scales):
    return unpack_weight(words.reshape(words.shape[0], 128, -1, 2), scales, "e2m1")


LQ, LK, D, H, DK, DV = 8192, 1024, 128, 8, 128, 128
HV = H * DV
LN_EPS = 1e-5


def setup_inputs():
    s = mx_kscale(HV)
    attn_out = bf(np.random.standard_normal((H, LQ, DV)) * 0.7 * s.reshape(H, DV)[:, None, :])
    residual = bf(np.random.standard_normal((LQ, D)))
    words, scales = pack4(np.random.standard_normal((HV, D)) / np.sqrt(HV) / s[:, None])
    proj_b = bf(np.random.standard_normal(D) * 0.3)
    ln_g = bf(1.0 + 0.1 * np.random.standard_normal(D))
    ln_b = bf(0.1 * np.random.standard_normal(D))
    return {"attn_out": attn_out,
            "residual": residual,
            "proj_w_words": words,
            "proj_w_scales": scales,
            "proj_b": proj_b,
            "ln_g": ln_g,
            "ln_b": ln_b}


def reference(attn_out, residual, proj_w_words, proj_w_scales, proj_b, ln_g, ln_b):
    x = f64(attn_out).transpose(1, 0, 2).reshape(LQ, HV)
    y = (mxq(x, 1, "e4m3") @ unpack4(proj_w_words, proj_w_scales)) + f64(proj_b) + f64(residual)
    mu = y.mean(-1, keepdims=True)
    var = ((y - mu) ** 2).mean(-1, keepdims=True)
    return (y - mu) / np.sqrt(var + LN_EPS) * f64(ln_g) + f64(ln_b)

@@ -1,0 +1,220 @@
+from contextlib import ExitStack
+
+import concourse.mybir as mybir
+from concourse.masks import make_identity
+
+F32 = mybir.dt.float32
+BF16 = mybir.dt.bfloat16
+I32 = mybir.dt.int32
+U32 = mybir.dt.uint32
+U8 = mybir.dt.uint8
+FP8X4 = mybir.dt.float8_e4m3fn_x4
+FP4X4 = mybir.dt.float4_e2m1fn_x4
+ADD = mybir.AluOpType.add
+MULT = mybir.AluOpType.mult
+FUNC = mybir.ActivationFunctionType
+
+P = 128
+TOKENS = 8192
+HEADS = 8
+HEAD_DIM = 128
+D_OUT = 128
+LN_EPS = 1e-5
+SLOTS = TOKENS // P
+PASSES = 2
+HEADS_PER_PASS = HEADS // PASSES
+PAIRS = HEAD_DIM // 2
+QUADS = HEAD_DIM // 4
+GROUP = 4
+N_GROUPS = SLOTS // GROUP
+LOADS_AHEAD = 4
+SCALAR_QUARTERS = 1
+
+FLOPS = 2 * TOKENS * HEADS * HEAD_DIM * D_OUT
+
+
+def tile_multiheadattention_pb_t_kernel(
+    tc, attn_out, residual, proj_w_words, proj_w_scales, proj_b, ln_g, ln_b, out
+):
+    nc = tc.nc
+    x_by_slot = attn_out.rearrange("h (p t) j -> p h t j", p=P)
+    r_by_slot = residual.rearrange("(p t) d -> p t d", p=P)
+    out_by_slot = out.rearrange("(p t) d -> p t d", p=P)
+
+    with ExitStack() as stack:
+        const = stack.enter_context(tc.tile_pool(name="const", bufs=1))
+        x_pool = stack.enter_context(tc.tile_pool(name="x", bufs=LOADS_AHEAD + 2))
+        sort_pool = stack.enter_context(tc.tile_pool(name="sort", bufs=3))
+        quant_pool = stack.enter_context(tc.tile_pool(name="quant", bufs=3))
+        norm_pool = stack.enter_context(tc.tile_pool(name="norm", bufs=4))
+        turned_psum = stack.enter_context(tc.psum_pool(name="turned", bufs=6))
+        acc_psum = stack.enter_context(tc.psum_pool(name="acc", bufs=2))
+
+        w_words = const.tile([P, PASSES, 2 * D_OUT], U8, align_bytes=64)
+        w_scales = const.tile([P, PASSES, D_OUT], U8, align_bytes=64)
+        nc.vector.memset(w_scales[:].bitcast(I32), 0)
+        identity = const.tile([P, P], F32)
+        make_identity(nc, identity[:])
+        eps = const.tile([P, 1], F32)
+        nc.vector.memset(eps[:], LN_EPS)
+        bias_rows = const.tile([P, D_OUT], BF16)
+        gain_rows = const.tile([P, D_OUT], BF16)
+        shift_rows = const.tile([P, D_OUT], BF16)
+        r_all = const.tile([P, SLOTS, D_OUT], BF16)
+
+        x_raw = {}
+        x_sorted = {}
+        x_grouped = {}
+        acc = {}
+        r_biased = {}
+        centred = {}
+        std = {}
+
+        def load(i):
+            raw = x_pool.tile([P, HEADS, GROUP, HEAD_DIM], BF16)
+            nc.sync.dma_start(out=raw[:], in_=x_by_slot[:, :, GROUP * i : GROUP * (i + 1), :])
+            x_raw[i] = raw
+
+        def sort(i):
+            words = x_raw[i][:].bitcast(F32)
+            sorted_words = sort_pool.tile([P, PASSES, 2, GROUP, P], F32)
+            for g in range(PASSES):
+                for u in range(2):
+                    src = words[:, HEADS_PER_PASS * g : HEADS_PER_PASS * (g + 1), :, u:PAIRS:2]
+                    src = src.rearrange("p h t q -> p t h q")
+                    dst = sorted_words[:, g, u, :, :].rearrange("p t (h q) -> p t h q", q=QUADS)
+                    if 2 * g + u < 2 * PASSES - SCALAR_QUARTERS:
+                        nc.vector.tensor_copy(out=dst, in_=src)
+                    else:
+                        nc.scalar.copy(out=dst, in_=src)
+            x_sorted[i] = sorted_words
+
+        def turn(i):
+            grouped = quant_pool.tile([P, GROUP, PASSES, P, 4], BF16, align_bytes=64)
+            for t in range(GROUP):
+                turned = turned_psum.tile([P, PASSES, 2, P], F32)
+                for g in range(PASSES):
+                    for u in range(2):
+                        nc.tensor.transpose(turned[:, g, u, :], x_sorted[i][:, g, u, t, :], identity[:])
+                nc.scalar.copy(
+                    out=grouped[:, t].bitcast(F32), in_=turned[:].rearrange("p g u m -> p g m u")
+                )
+            x_grouped[i] = grouped
+
+        def add_bias(i):
+            biased = norm_pool.tile([P, GROUP, D_OUT], F32)
+            nc.gpsimd.tensor_tensor(
+                out=biased[:],
+                in0=r_all[:, GROUP * i : GROUP * (i + 1), :],
+                in1=bias_rows[:].unsqueeze(1).to_broadcast([P, GROUP, D_OUT]),
+                op=ADD,
+            )
+            r_biased[i] = biased
+
+        def multiply(i):
+            codes = quant_pool.tile([P, GROUP, PASSES, P], U32, align_bytes=64)
+            scales = quant_pool.tile([P, GROUP, PASSES, P], U8, align_bytes=64)
+            nc.vector.quantize_mx(
+                out=codes[:].rearrange("p t g m -> p (t g m)").bitcast(FP8X4),
+                scales=scales[:].rearrange("p t g m -> p (t g m)"),
+                in_=x_grouped[i][:].rearrange("p t g m k -> p (t g m k)"),
+            )
+            products = acc_psum.tile([P, GROUP, D_OUT], F32)
+            for t in range(GROUP):
+                for g in range(PASSES):
+                    nc.tensor.matmul_mx(
+                        out=products[:, t, :],
+                        lhsT=codes[:, t, g, :].bitcast(FP8X4),
+                        lhsT_scale=scales[:, t, g, :],
+                        rhs=w_words[:, g, :].bitcast(FP4X4),
+                        rhs_scale=w_scales[:, g, :],
+                        start=(g == 0),
+                        stop=(g == PASSES - 1),
+                    )
+            acc[i] = products
+
+        def statistics(i):
+            y = norm_pool.tile([P, GROUP, D_OUT], F32)
+            sums = norm_pool.tile([P, GROUP], F32)
+            for t in range(GROUP):
+                nc.vector.scalar_tensor_tensor(
+                    out=y[:, t, :],
+                    in0=acc[i][:, t, :],
+                    scalar=1.0,
+                    in1=r_biased[i][:, t, :],
+                    op0=MULT,
+                    op1=ADD,
+                    accum_out=sums[:, t : t + 1],
+                )
+            minus_mean = norm_pool.tile([P, GROUP], F32)
+            nc.vector.tensor_scalar_mul(out=minus_mean[:], in0=sums[:], scalar1=-1.0 / D_OUT)
+            squares = norm_pool.tile([P, D_OUT], F32)
+            square_sums = norm_pool.tile([P, GROUP], F32)
+            for t in range(GROUP):
+                nc.scalar.activation(
+                    out=squares[:],
+                    in_=y[:, t, :],
+                    func=FUNC.Square,
+                    bias=minus_mean[:, t : t + 1],
+                    scale=1.0,
+                    accum_out=square_sums[:, t : t + 1],
+                )
+            deviation = norm_pool.tile([P, GROUP], F32)
+            nc.scalar.activation(
+                out=deviation[:], in_=square_sums[:], func=FUNC.Sqrt, bias=eps[:, 0:1], scale=1.0 / D_OUT
+            )
+            gained = norm_pool.tile([P, GROUP, D_OUT], F32)
+            for t in range(GROUP):
+                nc.vector.scalar_tensor_tensor(
+                    out=gained[:, t, :],
+                    in0=y[:, t, :],
+                    scalar=minus_mean[:, t : t + 1],
+                    in1=gain_rows[:],
+                    op0=ADD,
+                    op1=MULT,
+                )
+            centred[i] = gained
+            std[i] = deviation
+
+        def finish(i):
+            inverse = norm_pool.tile([P, GROUP], F32)
+            nc.vector.reciprocal(out=inverse[:], in_=std[i][:])
+            result = norm_pool.tile([P, GROUP, D_OUT], F32)
+            for t in range(GROUP):
+                nc.vector.scalar_tensor_tensor(
+                    out=result[:, t, :],
+                    in0=centred[i][:, t, :],
+                    scalar=inverse[:, t : t + 1],
+                    in1=shift_rows[:],
+                    op0=MULT,
+                    op1=ADD,
+                )
+            nc.sync.dma_start(out=out_by_slot[:, GROUP * i : GROUP * (i + 1), :], in_=result[:])
+
+        stages = [sort, turn, multiply, statistics, finish]
+        load(0)
+        nc.sync.dma_start(
+            out=w_words[:].bitcast(I32), in_=proj_w_words.rearrange("g p b -> p g b").bitcast(I32)
+        )
+        for quadrant in range(4):
+            nc.sync.dma_start(
+                out=w_scales[32 * quadrant : 32 * quadrant + 4].bitcast(I32),
+                in_=proj_w_scales[:, 4 * quadrant : 4 * quadrant + 4, :]
+                .rearrange("g r n -> r g n")
+                .bitcast(I32),
+            )
+        load(1)
+        nc.sync.dma_start(out=bias_rows[:], in_=proj_b.partition_broadcast(P))
+        nc.sync.dma_start(out=gain_rows[:], in_=ln_g.partition_broadcast(P))
+        nc.sync.dma_start(out=shift_rows[:], in_=ln_b.partition_broadcast(P))
+        nc.sync.dma_start(out=r_all[:], in_=r_by_slot)
+        for i in range(2, LOADS_AHEAD):
+            load(i)
+        for step in range(N_GROUPS + len(stages) - 1):
+            if step + LOADS_AHEAD < N_GROUPS:
+                load(step + LOADS_AHEAD)
+            if step < N_GROUPS:
+                add_bias(step)
+            for lag, stage in enumerate(stages):
+                if 0 <= step - lag < N_GROUPS:
+                    stage(step - lag)

@@ -28,7 +28,7 @@ QUADS = HEAD_DIM // 4
 GROUP = 4
 N_GROUPS = SLOTS // GROUP
 LOADS_AHEAD = 4
-SCALAR_QUARTERS = 1
+SCALAR_QUARTERS = 2
 
 FLOPS = 2 * TOKENS * HEADS * HEAD_DIM * D_OUT
 
@@ -46,7 +46,7 @@ def tile_multiheadattention_pb_t_kernel(
         x_pool = stack.enter_context(tc.tile_pool(name="x", bufs=LOADS_AHEAD + 2))
         sort_pool = stack.enter_context(tc.tile_pool(name="sort", bufs=3))
         quant_pool = stack.enter_context(tc.tile_pool(name="quant", bufs=3))
-        norm_pool = stack.enter_context(tc.tile_pool(name="norm", bufs=4))
+        norm_pool = stack.enter_context(tc.tile_pool(name="norm", bufs=5))
         turned_psum = stack.enter_context(tc.psum_pool(name="turned", bufs=6))
         acc_psum = stack.enter_context(tc.psum_pool(name="acc", bufs=2))
 
@@ -67,6 +67,8 @@ def tile_multiheadattention_pb_t_kernel(
         x_grouped = {}
         acc = {}
         r_biased = {}
+        summed = {}
+        shift = {}
         centred = {}
         std = {}
 
@@ -103,7 +105,7 @@ def tile_multiheadattention_pb_t_kernel(
 
         def add_bias(i):
             biased = norm_pool.tile([P, GROUP, D_OUT], F32)
-            nc.gpsimd.tensor_tensor(
+            nc.vector.tensor_tensor(
                 out=biased[:],
                 in0=r_all[:, GROUP * i : GROUP * (i + 1), :],
                 in1=bias_rows[:].unsqueeze(1).to_broadcast([P, GROUP, D_OUT]),
@@ -133,7 +135,7 @@ def tile_multiheadattention_pb_t_kernel(
                     )
             acc[i] = products
 
-        def statistics(i):
+        def add(i):
             y = norm_pool.tile([P, GROUP, D_OUT], F32)
             sums = norm_pool.tile([P, GROUP], F32)
             for t in range(GROUP):
@@ -148,21 +150,6 @@ def tile_multiheadattention_pb_t_kernel(
                 )
             minus_mean = norm_pool.tile([P, GROUP], F32)
             nc.vector.tensor_scalar_mul(out=minus_mean[:], in0=sums[:], scalar1=-1.0 / D_OUT)
-            squares = norm_pool.tile([P, D_OUT], F32)
-            square_sums = norm_pool.tile([P, GROUP], F32)
-            for t in range(GROUP):
-                nc.scalar.activation(
-                    out=squares[:],
-                    in_=y[:, t, :],
-                    func=FUNC.Square,
-                    bias=minus_mean[:, t : t + 1],
-                    scale=1.0,
-                    accum_out=square_sums[:, t : t + 1],
-                )
-            deviation = norm_pool.tile([P, GROUP], F32)
-            nc.scalar.activation(
-                out=deviation[:], in_=square_sums[:], func=FUNC.Sqrt, bias=eps[:, 0:1], scale=1.0 / D_OUT
-            )
             gained = norm_pool.tile([P, GROUP, D_OUT], F32)
             for t in range(GROUP):
                 nc.vector.scalar_tensor_tensor(
@@ -173,7 +160,26 @@ def tile_multiheadattention_pb_t_kernel(
                     op0=ADD,
                     op1=MULT,
                 )
+            summed[i] = y
+            shift[i] = minus_mean
             centred[i] = gained
+
+        def spread(i):
+            squares = norm_pool.tile([P, D_OUT], F32)
+            square_sums = norm_pool.tile([P, GROUP], F32)
+            for t in range(GROUP):
+                nc.scalar.activation(
+                    out=squares[:],
+                    in_=summed[i][:, t, :],
+                    func=FUNC.Square,
+                    bias=shift[i][:, t : t + 1],
+                    scale=1.0,
+                    accum_out=square_sums[:, t : t + 1],
+                )
+            deviation = norm_pool.tile([P, GROUP], F32)
+            nc.scalar.activation(
+                out=deviation[:], in_=square_sums[:], func=FUNC.Sqrt, bias=eps[:, 0:1], scale=1.0 / D_OUT
+            )
             std[i] = deviation
 
         def finish(i):
@@ -191,7 +197,7 @@ def tile_multiheadattention_pb_t_kernel(
                 )
             nc.sync.dma_start(out=out_by_slot[:, GROUP * i : GROUP * (i + 1), :], in_=result[:])
 
-        stages = [sort, turn, multiply, statistics, finish]
+        stages = [sort, turn, multiply, add, spread, finish]
         load(0)
         nc.sync.dma_start(
             out=w_words[:].bitcast(I32), in_=proj_w_words.rearrange("g p b -> p g b").bitcast(I32)
@@ -213,8 +219,8 @@ def tile_multiheadattention_pb_t_kernel(
         for step in range(N_GROUPS + len(stages) - 1):
             if step + LOADS_AHEAD < N_GROUPS:
                 load(step + LOADS_AHEAD)
-            if step < N_GROUPS:
-                add_bias(step)
+            if 0 <= step - 2 < N_GROUPS:
+                add_bias(step - 2)
             for lag, stage in enumerate(stages):
                 if 0 <= step - lag < N_GROUPS:
                     stage(step - lag)

@@ -28,7 +28,7 @@ QUADS = HEAD_DIM // 4
 GROUP = 4
 N_GROUPS = SLOTS // GROUP
 LOADS_AHEAD = 4
-SCALAR_QUARTERS = 2
+SCALAR_QUARTERS = 1
 
 FLOPS = 2 * TOKENS * HEADS * HEAD_DIM * D_OUT
 
@@ -46,7 +46,7 @@ def tile_multiheadattention_pb_t_kernel(
         x_pool = stack.enter_context(tc.tile_pool(name="x", bufs=LOADS_AHEAD + 2))
         sort_pool = stack.enter_context(tc.tile_pool(name="sort", bufs=3))
         quant_pool = stack.enter_context(tc.tile_pool(name="quant", bufs=3))
-        norm_pool = stack.enter_context(tc.tile_pool(name="norm", bufs=5))
+        norm_pool = stack.enter_context(tc.tile_pool(name="norm", bufs=4))
         turned_psum = stack.enter_context(tc.psum_pool(name="turned", bufs=6))
         acc_psum = stack.enter_context(tc.psum_pool(name="acc", bufs=2))
 
@@ -57,9 +57,14 @@ def tile_multiheadattention_pb_t_kernel(
         make_identity(nc, identity[:])
         eps = const.tile([P, 1], F32)
         nc.vector.memset(eps[:], LN_EPS)
-        bias_rows = const.tile([P, D_OUT], BF16)
-        gain_rows = const.tile([P, D_OUT], BF16)
-        shift_rows = const.tile([P, D_OUT], BF16)
+        vector_rows = const.tile([P, GROUP, D_OUT], BF16)
+        nc.vector.memset(vector_rows[:], 0.0)
+        ones = const.tile([P, P], BF16)
+        nc.vector.memset(ones[:], 1.0)
+        repeated = const.tile([P, GROUP, D_OUT], F32)
+        bias_rows = repeated[:, 0, :]
+        gain_rows = repeated[:, 1, :]
+        shift_rows = repeated[:, 2, :]
         r_all = const.tile([P, SLOTS, D_OUT], BF16)
 
         x_raw = {}
@@ -67,8 +72,6 @@ def tile_multiheadattention_pb_t_kernel(
         x_grouped = {}
         acc = {}
         r_biased = {}
-        summed = {}
-        shift = {}
         centred = {}
         std = {}
 
@@ -105,10 +108,10 @@ def tile_multiheadattention_pb_t_kernel(
 
         def add_bias(i):
             biased = norm_pool.tile([P, GROUP, D_OUT], F32)
-            nc.vector.tensor_tensor(
+            nc.gpsimd.tensor_tensor(
                 out=biased[:],
                 in0=r_all[:, GROUP * i : GROUP * (i + 1), :],
-                in1=bias_rows[:].unsqueeze(1).to_broadcast([P, GROUP, D_OUT]),
+                in1=bias_rows.unsqueeze(1).to_broadcast([P, GROUP, D_OUT]),
                 op=ADD,
             )
             r_biased[i] = biased
@@ -121,7 +124,7 @@ def tile_multiheadattention_pb_t_kernel(
                 scales=scales[:].rearrange("p t g m -> p (t g m)"),
                 in_=x_grouped[i][:].rearrange("p t g m k -> p (t g m k)"),
             )
-            products = acc_psum.tile([P, GROUP, D_OUT], F32)
+            products = acc_psum.tile([P, GROUP, D_OUT], F32, tag="products")
             for t in range(GROUP):
                 for g in range(PASSES):
                     nc.tensor.matmul_mx(
@@ -135,7 +138,7 @@ def tile_multiheadattention_pb_t_kernel(
                     )
             acc[i] = products
 
-        def add(i):
+        def statistics(i):
             y = norm_pool.tile([P, GROUP, D_OUT], F32)
             sums = norm_pool.tile([P, GROUP], F32)
             for t in range(GROUP):
@@ -150,29 +153,14 @@ def tile_multiheadattention_pb_t_kernel(
                 )
             minus_mean = norm_pool.tile([P, GROUP], F32)
             nc.vector.tensor_scalar_mul(out=minus_mean[:], in0=sums[:], scalar1=-1.0 / D_OUT)
-            gained = norm_pool.tile([P, GROUP, D_OUT], F32)
-            for t in range(GROUP):
-                nc.vector.scalar_tensor_tensor(
-                    out=gained[:, t, :],
-                    in0=y[:, t, :],
-                    scalar=minus_mean[:, t : t + 1],
-                    in1=gain_rows[:],
-                    op0=ADD,
-                    op1=MULT,
-                )
-            summed[i] = y
-            shift[i] = minus_mean
-            centred[i] = gained
-
-        def spread(i):
             squares = norm_pool.tile([P, D_OUT], F32)
             square_sums = norm_pool.tile([P, GROUP], F32)
             for t in range(GROUP):
                 nc.scalar.activation(
                     out=squares[:],
-                    in_=summed[i][:, t, :],
+                    in_=y[:, t, :],
                     func=FUNC.Square,
-                    bias=shift[i][:, t : t + 1],
+                    bias=minus_mean[:, t : t + 1],
                     scale=1.0,
                     accum_out=square_sums[:, t : t + 1],
                 )
@@ -180,6 +168,17 @@ def tile_multiheadattention_pb_t_kernel(
             nc.scalar.activation(
                 out=deviation[:], in_=square_sums[:], func=FUNC.Sqrt, bias=eps[:, 0:1], scale=1.0 / D_OUT
             )
+            gained = norm_pool.tile([P, GROUP, D_OUT], F32)
+            for t in range(GROUP):
+                nc.vector.scalar_tensor_tensor(
+                    out=gained[:, t, :],
+                    in0=y[:, t, :],
+                    scalar=minus_mean[:, t : t + 1],
+                    in1=gain_rows,
+                    op0=ADD,
+                    op1=MULT,
+                )
+            centred[i] = gained
             std[i] = deviation
 
         def finish(i):
@@ -191,13 +190,13 @@ def tile_multiheadattention_pb_t_kernel(
                     out=result[:, t, :],
                     in0=centred[i][:, t, :],
                     scalar=inverse[:, t : t + 1],
-                    in1=shift_rows[:],
+                    in1=shift_rows,
                     op0=MULT,
                     op1=ADD,
                 )
             nc.sync.dma_start(out=out_by_slot[:, GROUP * i : GROUP * (i + 1), :], in_=result[:])
 
-        stages = [sort, turn, multiply, add, spread, finish]
+        stages = [sort, turn, multiply, statistics, finish]
         load(0)
         nc.sync.dma_start(
             out=w_words[:].bitcast(I32), in_=proj_w_words.rearrange("g p b -> p g b").bitcast(I32)
@@ -209,18 +208,20 @@ def tile_multiheadattention_pb_t_kernel(
                 .rearrange("g r n -> r g n")
                 .bitcast(I32),
             )
+        for row, vector in enumerate([proj_b, ln_g, ln_b]):
+            nc.sync.dma_start(out=vector_rows[0:1, row, :], in_=vector.rearrange("(o d) -> o d", o=1))
         load(1)
-        nc.sync.dma_start(out=bias_rows[:], in_=proj_b.partition_broadcast(P))
-        nc.sync.dma_start(out=gain_rows[:], in_=ln_g.partition_broadcast(P))
-        nc.sync.dma_start(out=shift_rows[:], in_=ln_b.partition_broadcast(P))
         nc.sync.dma_start(out=r_all[:], in_=r_by_slot)
         for i in range(2, LOADS_AHEAD):
             load(i)
+        repeated_psum = acc_psum.tile([P, GROUP, D_OUT], F32, tag="products")
+        nc.tensor.matmul(out=repeated_psum[:], lhsT=ones[:], rhs=vector_rows[:], start=True, stop=True)
+        nc.vector.tensor_copy(out=repeated[:], in_=repeated_psum[:])
         for step in range(N_GROUPS + len(stages) - 1):
             if step + LOADS_AHEAD < N_GROUPS:
                 load(step + LOADS_AHEAD)
-            if 0 <= step - 2 < N_GROUPS:
-                add_bias(step - 2)
+            if step < N_GROUPS:
+                add_bias(step)
             for lag, stage in enumerate(stages):
                 if 0 <= step - lag < N_GROUPS:
                     stage(step - lag)

@@ -46,7 +46,7 @@ def tile_multiheadattention_pb_t_kernel(
         x_pool = stack.enter_context(tc.tile_pool(name="x", bufs=LOADS_AHEAD + 2))
         sort_pool = stack.enter_context(tc.tile_pool(name="sort", bufs=3))
         quant_pool = stack.enter_context(tc.tile_pool(name="quant", bufs=3))
-        norm_pool = stack.enter_context(tc.tile_pool(name="norm", bufs=4))
+        norm_pool = stack.enter_context(tc.tile_pool(name="norm", bufs=5))
         turned_psum = stack.enter_context(tc.psum_pool(name="turned", bufs=6))
         acc_psum = stack.enter_context(tc.psum_pool(name="acc", bufs=2))
 
@@ -65,34 +65,44 @@ def tile_multiheadattention_pb_t_kernel(
         bias_rows = repeated[:, 0, :]
         gain_rows = repeated[:, 1, :]
         shift_rows = repeated[:, 2, :]
-        r_all = const.tile([P, SLOTS, D_OUT], BF16)
 
         x_raw = {}
+        r_raw = {}
         x_sorted = {}
         x_grouped = {}
+        x_codes = {}
+        x_scales = {}
+        summed = {}
+        sum_of = {}
+        shift = {}
+        inverse_of = {}
         acc = {}
         r_biased = {}
         centred = {}
         std = {}
 
         def load(i):
+            slots = slice(GROUP * i, GROUP * (i + 1))
             raw = x_pool.tile([P, HEADS, GROUP, HEAD_DIM], BF16)
-            nc.sync.dma_start(out=raw[:], in_=x_by_slot[:, :, GROUP * i : GROUP * (i + 1), :])
+            nc.sync.dma_start(out=raw[:], in_=x_by_slot[:, :, slots, :])
             x_raw[i] = raw
+            rest = x_pool.tile([P, GROUP, D_OUT], BF16)
+            nc.sync.dma_start(out=rest[:], in_=r_by_slot[:, slots, :])
+            r_raw[i] = rest
 
-        def sort(i):
+        def sort(i, quarter):
+            if i not in x_sorted:
+                sorted_words = sort_pool.tile([P, PASSES, 2, GROUP, P], F32)
+                x_sorted[i] = sorted_words
+            g, u = divmod(quarter, 2)
             words = x_raw[i][:].bitcast(F32)
-            sorted_words = sort_pool.tile([P, PASSES, 2, GROUP, P], F32)
-            for g in range(PASSES):
-                for u in range(2):
-                    src = words[:, HEADS_PER_PASS * g : HEADS_PER_PASS * (g + 1), :, u:PAIRS:2]
-                    src = src.rearrange("p h t q -> p t h q")
-                    dst = sorted_words[:, g, u, :, :].rearrange("p t (h q) -> p t h q", q=QUADS)
-                    if 2 * g + u < 2 * PASSES - SCALAR_QUARTERS:
-                        nc.vector.tensor_copy(out=dst, in_=src)
-                    else:
-                        nc.scalar.copy(out=dst, in_=src)
-            x_sorted[i] = sorted_words
+            src = words[:, HEADS_PER_PASS * g : HEADS_PER_PASS * (g + 1), :, u:PAIRS:2]
+            src = src.rearrange("p h t q -> p t h q")
+            dst = x_sorted[i][:, g, u, :, :].rearrange("p t (h q) -> p t h q", q=QUADS)
+            if quarter < 2 * PASSES - SCALAR_QUARTERS:
+                nc.vector.tensor_copy(out=dst, in_=src)
+            else:
+                nc.scalar.copy(out=dst, in_=src)
 
         def turn(i):
             grouped = quant_pool.tile([P, GROUP, PASSES, P, 4], BF16, align_bytes=64)
@@ -110,13 +120,13 @@ def tile_multiheadattention_pb_t_kernel(
             biased = norm_pool.tile([P, GROUP, D_OUT], F32)
             nc.gpsimd.tensor_tensor(
                 out=biased[:],
-                in0=r_all[:, GROUP * i : GROUP * (i + 1), :],
+                in0=r_raw[i][:],
                 in1=bias_rows.unsqueeze(1).to_broadcast([P, GROUP, D_OUT]),
                 op=ADD,
             )
             r_biased[i] = biased
 
-        def multiply(i):
+        def quantise(i):
             codes = quant_pool.tile([P, GROUP, PASSES, P], U32, align_bytes=64)
             scales = quant_pool.tile([P, GROUP, PASSES, P], U8, align_bytes=64)
             nc.vector.quantize_mx(
@@ -124,6 +134,12 @@ def tile_multiheadattention_pb_t_kernel(
                 scales=scales[:].rearrange("p t g m -> p (t g m)"),
                 in_=x_grouped[i][:].rearrange("p t g m k -> p (t g m k)"),
             )
+            x_codes[i] = codes
+            x_scales[i] = scales
+
+        def multiply(i):
+            codes = x_codes[i]
+            scales = x_scales[i]
             products = acc_psum.tile([P, GROUP, D_OUT], F32, tag="products")
             for t in range(GROUP):
                 for g in range(PASSES):
@@ -138,7 +154,7 @@ def tile_multiheadattention_pb_t_kernel(
                     )
             acc[i] = products
 
-        def statistics(i):
+        def add_residual(i):
             y = norm_pool.tile([P, GROUP, D_OUT], F32)
             sums = norm_pool.tile([P, GROUP], F32)
             for t in range(GROUP):
@@ -151,16 +167,36 @@ def tile_multiheadattention_pb_t_kernel(
                     op1=ADD,
                     accum_out=sums[:, t : t + 1],
                 )
+            summed[i] = y
+            sum_of[i] = sums
+
+        def mean(i):
             minus_mean = norm_pool.tile([P, GROUP], F32)
-            nc.vector.tensor_scalar_mul(out=minus_mean[:], in0=sums[:], scalar1=-1.0 / D_OUT)
+            nc.vector.tensor_scalar_mul(out=minus_mean[:], in0=sum_of[i][:], scalar1=-1.0 / D_OUT)
+            shift[i] = minus_mean
+
+        def centre(i):
+            gained = norm_pool.tile([P, GROUP, D_OUT], F32)
+            for t in range(GROUP):
+                nc.vector.scalar_tensor_tensor(
+                    out=gained[:, t, :],
+                    in0=summed[i][:, t, :],
+                    scalar=shift[i][:, t : t + 1],
+                    in1=gain_rows,
+                    op0=ADD,
+                    op1=MULT,
+                )
+            centred[i] = gained
+
+        def spread(i):
             squares = norm_pool.tile([P, D_OUT], F32)
             square_sums = norm_pool.tile([P, GROUP], F32)
             for t in range(GROUP):
                 nc.scalar.activation(
                     out=squares[:],
-                    in_=y[:, t, :],
+                    in_=summed[i][:, t, :],
                     func=FUNC.Square,
-                    bias=minus_mean[:, t : t + 1],
+                    bias=shift[i][:, t : t + 1],
                     scale=1.0,
                     accum_out=square_sums[:, t : t + 1],
                 )
@@ -168,60 +204,62 @@ def tile_multiheadattention_pb_t_kernel(
             nc.scalar.activation(
                 out=deviation[:], in_=square_sums[:], func=FUNC.Sqrt, bias=eps[:, 0:1], scale=1.0 / D_OUT
             )
-            gained = norm_pool.tile([P, GROUP, D_OUT], F32)
-            for t in range(GROUP):
-                nc.vector.scalar_tensor_tensor(
-                    out=gained[:, t, :],
-                    in0=y[:, t, :],
-                    scalar=minus_mean[:, t : t + 1],
-                    in1=gain_rows,
-                    op0=ADD,
-                    op1=MULT,
-                )
-            centred[i] = gained
             std[i] = deviation
 
-        def finish(i):
+        def invert(i):
             inverse = norm_pool.tile([P, GROUP], F32)
             nc.vector.reciprocal(out=inverse[:], in_=std[i][:])
+            inverse_of[i] = inverse
+
+        def finish(i):
             result = norm_pool.tile([P, GROUP, D_OUT], F32)
             for t in range(GROUP):
                 nc.vector.scalar_tensor_tensor(
                     out=result[:, t, :],
                     in0=centred[i][:, t, :],
-                    scalar=inverse[:, t : t + 1],
+                    scalar=inverse_of[i][:, t : t + 1],
                     in1=shift_rows,
                     op0=MULT,
                     op1=ADD,
                 )
             nc.sync.dma_start(out=out_by_slot[:, GROUP * i : GROUP * (i + 1), :], in_=result[:])
 
-        stages = [sort, turn, multiply, statistics, finish]
-        load(0)
-        nc.sync.dma_start(
-            out=w_words[:].bitcast(I32), in_=proj_w_words.rearrange("g p b -> p g b").bitcast(I32)
-        )
-        for quadrant in range(4):
+        def run(stage, i, *args):
+            if 0 <= i < N_GROUPS:
+                stage(i, *args)
+
+        with tc.manual_schedule():
+            load(0)
             nc.sync.dma_start(
-                out=w_scales[32 * quadrant : 32 * quadrant + 4].bitcast(I32),
-                in_=proj_w_scales[:, 4 * quadrant : 4 * quadrant + 4, :]
-                .rearrange("g r n -> r g n")
-                .bitcast(I32),
+                out=w_words[:].bitcast(I32), in_=proj_w_words.rearrange("g p b -> p g b").bitcast(I32)
             )
-        for row, vector in enumerate([proj_b, ln_g, ln_b]):
-            nc.sync.dma_start(out=vector_rows[0:1, row, :], in_=vector.rearrange("(o d) -> o d", o=1))
-        load(1)
-        nc.sync.dma_start(out=r_all[:], in_=r_by_slot)
-        for i in range(2, LOADS_AHEAD):
-            load(i)
-        repeated_psum = acc_psum.tile([P, GROUP, D_OUT], F32, tag="products")
-        nc.tensor.matmul(out=repeated_psum[:], lhsT=ones[:], rhs=vector_rows[:], start=True, stop=True)
-        nc.vector.tensor_copy(out=repeated[:], in_=repeated_psum[:])
-        for step in range(N_GROUPS + len(stages) - 1):
-            if step + LOADS_AHEAD < N_GROUPS:
-                load(step + LOADS_AHEAD)
-            if step < N_GROUPS:
-                add_bias(step)
-            for lag, stage in enumerate(stages):
-                if 0 <= step - lag < N_GROUPS:
-                    stage(step - lag)
+            for quadrant in range(4):
+                nc.sync.dma_start(
+                    out=w_scales[32 * quadrant : 32 * quadrant + 4].bitcast(I32),
+                    in_=proj_w_scales[:, 4 * quadrant : 4 * quadrant + 4, :]
+                    .rearrange("g r n -> r g n")
+                    .bitcast(I32),
+                )
+            for row, vector in enumerate([proj_b, ln_g, ln_b]):
+                nc.sync.dma_start(out=vector_rows[0:1, row, :], in_=vector.rearrange("(o d) -> o d", o=1))
+            for i in range(1, LOADS_AHEAD):
+                load(i)
+            repeated_psum = acc_psum.tile([P, GROUP, D_OUT], F32, tag="products")
+            nc.tensor.matmul(out=repeated_psum[:], lhsT=ones[:], rhs=vector_rows[:], start=True, stop=True)
+            nc.vector.tensor_copy(out=repeated[:], in_=repeated_psum[:])
+            for step in range(N_GROUPS + 5):
+                run(load, step + LOADS_AHEAD)
+                run(add_bias, step)
+                run(sort, step, 3)
+                run(turn, step - 1)
+                run(quantise, step - 2)
+                run(multiply, step - 2)
+                run(add_residual, step - 3)
+                run(sort, step, 0)
+                run(mean, step - 3)
+                run(sort, step, 1)
+                run(centre, step - 3)
+                run(spread, step - 4)
+                run(invert, step - 5)
+                run(sort, step, 2)
+                run(finish, step - 5)

@@ -21,14 +21,14 @@ HEAD_DIM = 128
 D_OUT = 128
 LN_EPS = 1e-5
 SLOTS = TOKENS // P
-PASSES = 2
-HEADS_PER_PASS = HEADS // PASSES
 PAIRS = HEAD_DIM // 2
 QUADS = HEAD_DIM // 4
+DUO = 2
+HEAD_DUOS = HEADS // DUO
 GROUP = 4
+SLOT_DUOS = GROUP // DUO
 N_GROUPS = SLOTS // GROUP
 LOADS_AHEAD = 4
-SCALAR_QUARTERS = 1
 
 FLOPS = 2 * TOKENS * HEADS * HEAD_DIM * D_OUT
 
@@ -44,14 +44,14 @@ def tile_multiheadattention_pb_t_kernel(
     with ExitStack() as stack:
         const = stack.enter_context(tc.tile_pool(name="const", bufs=1))
         x_pool = stack.enter_context(tc.tile_pool(name="x", bufs=LOADS_AHEAD + 2))
-        sort_pool = stack.enter_context(tc.tile_pool(name="sort", bufs=3))
         quant_pool = stack.enter_context(tc.tile_pool(name="quant", bufs=3))
         norm_pool = stack.enter_context(tc.tile_pool(name="norm", bufs=5))
         turned_psum = stack.enter_context(tc.psum_pool(name="turned", bufs=6))
         acc_psum = stack.enter_context(tc.psum_pool(name="acc", bufs=2))
 
-        w_words = const.tile([P, PASSES, 2 * D_OUT], U8, align_bytes=64)
-        w_scales = const.tile([P, PASSES, D_OUT], U8, align_bytes=64)
+        w_words = const.tile([P, HEAD_DUOS, DUO, 2 * D_OUT], U8, align_bytes=64)
+        nc.vector.memset(w_words[:].bitcast(I32), 0)
+        w_scales = const.tile([P, HEAD_DUOS, DUO, D_OUT], U8, align_bytes=64)
         nc.vector.memset(w_scales[:].bitcast(I32), 0)
         identity = const.tile([P, P], F32)
         make_identity(nc, identity[:])
@@ -68,7 +68,6 @@ def tile_multiheadattention_pb_t_kernel(
 
         x_raw = {}
         r_raw = {}
-        x_sorted = {}
         x_grouped = {}
         x_codes = {}
         x_scales = {}
@@ -82,38 +81,32 @@ def tile_multiheadattention_pb_t_kernel(
         std = {}
 
         def load(i):
-            slots = slice(GROUP * i, GROUP * (i + 1))
-            raw = x_pool.tile([P, HEADS, GROUP, HEAD_DIM], BF16)
-            nc.sync.dma_start(out=raw[:], in_=x_by_slot[:, :, slots, :])
+            raw = x_pool.tile([P, SLOT_DUOS, HEADS, DUO, HEAD_DIM], BF16)
+            for s in range(SLOT_DUOS):
+                first = GROUP * i + DUO * s
+                nc.sync.dma_start(out=raw[:, s], in_=x_by_slot[:, :, first : first + DUO, :])
             x_raw[i] = raw
             rest = x_pool.tile([P, GROUP, D_OUT], BF16)
-            nc.sync.dma_start(out=rest[:], in_=r_by_slot[:, slots, :])
+            nc.sync.dma_start(out=rest[:], in_=r_by_slot[:, GROUP * i : GROUP * (i + 1), :])
             r_raw[i] = rest
 
-        def sort(i, quarter):
-            if i not in x_sorted:
-                sorted_words = sort_pool.tile([P, PASSES, 2, GROUP, P], F32)
-                x_sorted[i] = sorted_words
-            g, u = divmod(quarter, 2)
-            words = x_raw[i][:].bitcast(F32)
-            src = words[:, HEADS_PER_PASS * g : HEADS_PER_PASS * (g + 1), :, u:PAIRS:2]
-            src = src.rearrange("p h t q -> p t h q")
-            dst = x_sorted[i][:, g, u, :, :].rearrange("p t (h q) -> p t h q", q=QUADS)
-            if quarter < 2 * PASSES - SCALAR_QUARTERS:
-                nc.vector.tensor_copy(out=dst, in_=src)
-            else:
-                nc.scalar.copy(out=dst, in_=src)
-
         def turn(i):
-            grouped = quant_pool.tile([P, GROUP, PASSES, P, 4], BF16, align_bytes=64)
-            for t in range(GROUP):
-                turned = turned_psum.tile([P, PASSES, 2, P], F32)
-                for g in range(PASSES):
-                    for u in range(2):
-                        nc.tensor.transpose(turned[:, g, u, :], x_sorted[i][:, g, u, t, :], identity[:])
-                nc.scalar.copy(
-                    out=grouped[:, t].bitcast(F32), in_=turned[:].rearrange("p g u m -> p g m u")
-                )
+            words = x_raw[i][:].bitcast(F32).rearrange("p s h t w -> p s (h t w)")
+            span = DUO * DUO * PAIRS
+            grouped = quant_pool.tile([P, SLOT_DUOS, HEAD_DUOS, P, 4], BF16, align_bytes=64)
+            for s in range(SLOT_DUOS):
+                for half in range(HEAD_DUOS // 2):
+                    turned = turned_psum.tile([P, 2, 2, P], F32)
+                    for k in range(2):
+                        d = 2 * half + k
+                        for u in range(2):
+                            nc.tensor.transpose(
+                                turned[:, k, u, :], words[:, s, span * d + u : span * (d + 1) : 2], identity[:]
+                            )
+                    nc.scalar.copy(
+                        out=grouped[:, s, 2 * half : 2 * half + 2].bitcast(F32),
+                        in_=turned[:].rearrange("p k u m -> p k m u"),
+                    )
             x_grouped[i] = grouped
 
         def add_bias(i):
@@ -127,31 +120,30 @@ def tile_multiheadattention_pb_t_kernel(
             r_biased[i] = biased
 
         def quantise(i):
-            codes = quant_pool.tile([P, GROUP, PASSES, P], U32, align_bytes=64)
-            scales = quant_pool.tile([P, GROUP, PASSES, P], U8, align_bytes=64)
+            codes = quant_pool.tile([P, SLOT_DUOS, HEAD_DUOS, P], U32, align_bytes=64)
+            scales = quant_pool.tile([P, SLOT_DUOS, HEAD_DUOS, P], U8, align_bytes=64)
             nc.vector.quantize_mx(
-                out=codes[:].rearrange("p t g m -> p (t g m)").bitcast(FP8X4),
-                scales=scales[:].rearrange("p t g m -> p (t g m)"),
-                in_=x_grouped[i][:].rearrange("p t g m k -> p (t g m k)"),
+                out=codes[:].rearrange("p s d m -> p (s d m)").bitcast(FP8X4),
+                scales=scales[:].rearrange("p s d m -> p (s d m)"),
+                in_=x_grouped[i][:].rearrange("p s d m k -> p (s d m k)"),
             )
             x_codes[i] = codes
             x_scales[i] = scales
 
         def multiply(i):
-            codes = x_codes[i]
-            scales = x_scales[i]
             products = acc_psum.tile([P, GROUP, D_OUT], F32, tag="products")
-            for t in range(GROUP):
-                for g in range(PASSES):
-                    nc.tensor.matmul_mx(
-                        out=products[:, t, :],
-                        lhsT=codes[:, t, g, :].bitcast(FP8X4),
-                        lhsT_scale=scales[:, t, g, :],
-                        rhs=w_words[:, g, :].bitcast(FP4X4),
-                        rhs_scale=w_scales[:, g, :],
-                        start=(g == 0),
-                        stop=(g == PASSES - 1),
-                    )
+            for s in range(SLOT_DUOS):
+                for t in range(DUO):
+                    for d in range(HEAD_DUOS):
+                        nc.tensor.matmul_mx(
+                            out=products[:, DUO * s + t, :],
+                            lhsT=x_codes[i][:, s, d, :].bitcast(FP8X4),
+                            lhsT_scale=x_scales[i][:, s, d, :],
+                            rhs=w_words[:, d, t, :].bitcast(FP4X4),
+                            rhs_scale=w_scales[:, d, t, :],
+                            start=(d == 0),
+                            stop=(d == HEAD_DUOS - 1),
+                        )
             acc[i] = products
 
         def add_residual(i):
@@ -228,38 +220,41 @@ def tile_multiheadattention_pb_t_kernel(
             if 0 <= i < N_GROUPS:
                 stage(i, *args)
 
+        def repeat_vectors():
+            repeated_psum = acc_psum.tile([P, GROUP, D_OUT], F32, tag="products")
+            nc.tensor.matmul(out=repeated_psum[:], lhsT=ones[:], rhs=vector_rows[:], start=True, stop=True)
+            nc.vector.tensor_copy(out=repeated[:], in_=repeated_psum[:])
+
         with tc.manual_schedule():
             load(0)
-            nc.sync.dma_start(
-                out=w_words[:].bitcast(I32), in_=proj_w_words.rearrange("g p b -> p g b").bitcast(I32)
-            )
-            for quadrant in range(4):
-                nc.sync.dma_start(
-                    out=w_scales[32 * quadrant : 32 * quadrant + 4].bitcast(I32),
-                    in_=proj_w_scales[:, 4 * quadrant : 4 * quadrant + 4, :]
-                    .rearrange("g r n -> r g n")
-                    .bitcast(I32),
-                )
+            words_by_duo = proj_w_words.rearrange("g (a h q) b -> h q (g a) b", h=DUO, q=QUADS)
+            scales_by_duo = proj_w_scales.rearrange("g (a h r) n -> h r (g a) n", h=DUO, r=QUADS // 8)
+            for h in range(DUO):
+                for t in range(DUO):
+                    quarter = QUADS * (DUO * h + t)
+                    nc.sync.dma_start(
+                        out=w_words[quarter : quarter + QUADS, :, t, :].bitcast(I32),
+                        in_=words_by_duo[h].bitcast(I32),
+                    )
+                    nc.sync.dma_start(
+                        out=w_scales[quarter : quarter + QUADS // 8, :, t, :].bitcast(I32),
+                        in_=scales_by_duo[h].bitcast(I32),
+                    )
             for row, vector in enumerate([proj_b, ln_g, ln_b]):
                 nc.sync.dma_start(out=vector_rows[0:1, row, :], in_=vector.rearrange("(o d) -> o d", o=1))
             for i in range(1, LOADS_AHEAD):
                 load(i)
-            repeated_psum = acc_psum.tile([P, GROUP, D_OUT], F32, tag="products")
-            nc.tensor.matmul(out=repeated_psum[:], lhsT=ones[:], rhs=vector_rows[:], start=True, stop=True)
-            nc.vector.tensor_copy(out=repeated[:], in_=repeated_psum[:])
             for step in range(N_GROUPS + 5):
                 run(load, step + LOADS_AHEAD)
+                run(spread, step - 3)
+                run(turn, step)
+                if step == 0:
+                    repeat_vectors()
                 run(add_bias, step)
-                run(sort, step, 3)
-                run(turn, step - 1)
-                run(quantise, step - 2)
-                run(multiply, step - 2)
-                run(add_residual, step - 3)
-                run(sort, step, 0)
-                run(mean, step - 3)
-                run(sort, step, 1)
+                run(quantise, step - 1)
+                run(multiply, step - 1)
                 run(centre, step - 3)
-                run(spread, step - 4)
-                run(invert, step - 5)
-                run(sort, step, 2)
+                run(add_residual, step - 2)
                 run(finish, step - 5)
+                run(mean, step - 2)
+                run(invert, step - 4)

@@ -46,7 +46,8 @@ def tile_multiheadattention_pb_t_kernel(
         x_pool = stack.enter_context(tc.tile_pool(name="x", bufs=LOADS_AHEAD + 2))
         quant_pool = stack.enter_context(tc.tile_pool(name="quant", bufs=3))
         norm_pool = stack.enter_context(tc.tile_pool(name="norm", bufs=5))
-        turned_psum = stack.enter_context(tc.psum_pool(name="turned", bufs=6))
+        turned_psum = stack.enter_context(tc.psum_pool(name="turned", bufs=5))
+        rows_psum = stack.enter_context(tc.psum_pool(name="rows", bufs=1))
         acc_psum = stack.enter_context(tc.psum_pool(name="acc", bufs=2))
 
         w_words = const.tile([P, HEAD_DUOS, DUO, 2 * D_OUT], U8, align_bytes=64)
@@ -61,8 +62,9 @@ def tile_multiheadattention_pb_t_kernel(
         nc.vector.memset(vector_rows[:], 0.0)
         ones = const.tile([P, P], BF16)
         nc.vector.memset(ones[:], 1.0)
-        repeated = const.tile([P, GROUP, D_OUT], F32)
-        bias_rows = repeated[:, 0, :]
+        repeated = rows_psum.tile([P, GROUP, D_OUT], F32)
+        bias_copy = const.tile([P, D_OUT], F32)
+        bias_rows = bias_copy[:]
         gain_rows = repeated[:, 1, :]
         shift_rows = repeated[:, 2, :]
 
@@ -221,9 +223,8 @@ def tile_multiheadattention_pb_t_kernel(
                 stage(i, *args)
 
         def repeat_vectors():
-            repeated_psum = acc_psum.tile([P, GROUP, D_OUT], F32, tag="products")
-            nc.tensor.matmul(out=repeated_psum[:], lhsT=ones[:], rhs=vector_rows[:], start=True, stop=True)
-            nc.vector.tensor_copy(out=repeated[:], in_=repeated_psum[:])
+            nc.tensor.matmul(out=repeated[:], lhsT=ones[:], rhs=vector_rows[:], start=True, stop=True)
+            nc.vector.tensor_copy(out=bias_copy[:], in_=repeated[:, 0, :])
 
         with tc.manual_schedule():
             load(0)

@@ -25,10 +25,11 @@ PAIRS = HEAD_DIM // 2
 QUADS = HEAD_DIM // 4
 DUO = 2
 HEAD_DUOS = HEADS // DUO
-GROUP = 4
-SLOT_DUOS = GROUP // DUO
-N_GROUPS = SLOTS // GROUP
-LOADS_AHEAD = 4
+ROWS = 4
+GROUP_DUOS = [2] * 15 + [1, 1]
+N_GROUPS = len(GROUP_DUOS)
+FIRST_SLOT = [DUO * sum(GROUP_DUOS[:i]) for i in range(N_GROUPS)]
+LOADS_AHEAD = 6
 
 FLOPS = 2 * TOKENS * HEADS * HEAD_DIM * D_OUT
 
@@ -58,11 +59,11 @@ def tile_multiheadattention_pb_t_kernel(
         make_identity(nc, identity[:])
         eps = const.tile([P, 1], F32)
         nc.vector.memset(eps[:], LN_EPS)
-        vector_rows = const.tile([P, GROUP, D_OUT], BF16)
+        vector_rows = const.tile([P, ROWS, D_OUT], BF16)
         nc.vector.memset(vector_rows[:], 0.0)
         ones = const.tile([P, P], BF16)
         nc.vector.memset(ones[:], 1.0)
-        repeated = rows_psum.tile([P, GROUP, D_OUT], F32)
+        repeated = rows_psum.tile([P, ROWS, D_OUT], F32)
         bias_copy = const.tile([P, D_OUT], F32)
         bias_rows = bias_copy[:]
         gain_rows = repeated[:, 1, :]
@@ -80,25 +81,28 @@ def tile_multiheadattention_pb_t_kernel(
         acc = {}
         r_biased = {}
         centred = {}
-        std = {}
 
         def load(i):
-            raw = x_pool.tile([P, SLOT_DUOS, HEADS, DUO, HEAD_DIM], BF16)
-            for s in range(SLOT_DUOS):
-                first = GROUP * i + DUO * s
-                nc.sync.dma_start(out=raw[:, s], in_=x_by_slot[:, :, first : first + DUO, :])
+            duos = GROUP_DUOS[i]
+            raw = x_pool.tile([P, duos, HEADS, DUO, HEAD_DIM], BF16, tag="raw")
+            cuts = [0, 2, 4, HEADS] if i == 0 else [0, HEADS]
+            for s in range(duos):
+                first = FIRST_SLOT[i] + DUO * s
+                for a, b in zip(cuts[:-1], cuts[1:]):
+                    nc.sync.dma_start(out=raw[:, s, a:b], in_=x_by_slot[:, a:b, first : first + DUO, :])
             x_raw[i] = raw
-            rest = x_pool.tile([P, GROUP, D_OUT], BF16)
-            nc.sync.dma_start(out=rest[:], in_=r_by_slot[:, GROUP * i : GROUP * (i + 1), :])
+            rest = x_pool.tile([P, DUO * duos, D_OUT], BF16, tag="rest")
+            nc.sync.dma_start(out=rest[:], in_=r_by_slot[:, FIRST_SLOT[i] : FIRST_SLOT[i] + DUO * duos, :])
             r_raw[i] = rest
 
         def turn(i):
+            duos = GROUP_DUOS[i]
             words = x_raw[i][:].bitcast(F32).rearrange("p s h t w -> p s (h t w)")
             span = DUO * DUO * PAIRS
-            grouped = quant_pool.tile([P, SLOT_DUOS, HEAD_DUOS, P, 4], BF16, align_bytes=64)
-            for s in range(SLOT_DUOS):
+            grouped = quant_pool.tile([P, duos, HEAD_DUOS, P, 4], BF16, align_bytes=64, tag="grouped")
+            for s in range(duos):
                 for half in range(HEAD_DUOS // 2):
-                    turned = turned_psum.tile([P, 2, 2, P], F32)
+                    turned = turned_psum.tile([P, 2, 2, P], F32, tag="turned")
                     for k in range(2):
                         d = 2 * half + k
                         for u in range(2):
@@ -112,18 +116,20 @@ def tile_multiheadattention_pb_t_kernel(
             x_grouped[i] = grouped
 
         def add_bias(i):
-            biased = norm_pool.tile([P, GROUP, D_OUT], F32)
+            slots = DUO * GROUP_DUOS[i]
+            biased = norm_pool.tile([P, slots, D_OUT], F32, tag="biased")
             nc.gpsimd.tensor_tensor(
                 out=biased[:],
                 in0=r_raw[i][:],
-                in1=bias_rows.unsqueeze(1).to_broadcast([P, GROUP, D_OUT]),
+                in1=bias_rows.unsqueeze(1).to_broadcast([P, slots, D_OUT]),
                 op=ADD,
             )
             r_biased[i] = biased
 
         def quantise(i):
-            codes = quant_pool.tile([P, SLOT_DUOS, HEAD_DUOS, P], U32, align_bytes=64)
-            scales = quant_pool.tile([P, SLOT_DUOS, HEAD_DUOS, P], U8, align_bytes=64)
+            duos = GROUP_DUOS[i]
+            codes = quant_pool.tile([P, duos, HEAD_DUOS, P], U32, align_bytes=64, tag="codes")
+            scales = quant_pool.tile([P, duos, HEAD_DUOS, P], U8, align_bytes=64, tag="scales")
             nc.vector.quantize_mx(
                 out=codes[:].rearrange("p s d m -> p (s d m)").bitcast(FP8X4),
                 scales=scales[:].rearrange("p s d m -> p (s d m)"),
@@ -133,8 +139,9 @@ def tile_multiheadattention_pb_t_kernel(
             x_scales[i] = scales
 
         def multiply(i):
-            products = acc_psum.tile([P, GROUP, D_OUT], F32, tag="products")
-            for s in range(SLOT_DUOS):
+            duos = GROUP_DUOS[i]
+            products = acc_psum.tile([P, DUO * duos, D_OUT], F32, tag="products")
+            for s in range(duos):
                 for t in range(DUO):
                     for d in range(HEAD_DUOS):
                         nc.tensor.matmul_mx(
@@ -149,9 +156,10 @@ def tile_multiheadattention_pb_t_kernel(
             acc[i] = products
 
         def add_residual(i):
-            y = norm_pool.tile([P, GROUP, D_OUT], F32)
-            sums = norm_pool.tile([P, GROUP], F32)
-            for t in range(GROUP):
+            slots = DUO * GROUP_DUOS[i]
+            y = norm_pool.tile([P, slots, D_OUT], F32, tag="y")
+            sums = norm_pool.tile([P, slots], F32, tag="sums")
+            for t in range(slots):
                 nc.vector.scalar_tensor_tensor(
                     out=y[:, t, :],
                     in0=acc[i][:, t, :],
@@ -165,13 +173,14 @@ def tile_multiheadattention_pb_t_kernel(
             sum_of[i] = sums
 
         def mean(i):
-            minus_mean = norm_pool.tile([P, GROUP], F32)
-            nc.vector.tensor_scalar_mul(out=minus_mean[:], in0=sum_of[i][:], scalar1=-1.0 / D_OUT)
+            minus_mean = norm_pool.tile([P, DUO * GROUP_DUOS[i]], F32, tag="minus_mean")
+            nc.gpsimd.tensor_scalar_mul(out=minus_mean[:], in0=sum_of[i][:], scalar1=-1.0 / D_OUT)
             shift[i] = minus_mean
 
         def centre(i):
-            gained = norm_pool.tile([P, GROUP, D_OUT], F32)
-            for t in range(GROUP):
+            slots = DUO * GROUP_DUOS[i]
+            gained = norm_pool.tile([P, slots, D_OUT], F32, tag="gained")
+            for t in range(slots):
                 nc.vector.scalar_tensor_tensor(
                     out=gained[:, t, :],
                     in0=summed[i][:, t, :],
@@ -183,31 +192,32 @@ def tile_multiheadattention_pb_t_kernel(
             centred[i] = gained
 
         def spread(i):
-            squares = norm_pool.tile([P, D_OUT], F32)
-            square_sums = norm_pool.tile([P, GROUP], F32)
-            for t in range(GROUP):
+            slots = DUO * GROUP_DUOS[i]
+            squares = norm_pool.tile([P, D_OUT], F32, tag="squares")
+            square_sums = norm_pool.tile([P, slots], F32, tag="square_sums")
+            for t in range(slots):
                 nc.scalar.activation(
                     out=squares[:],
                     in_=summed[i][:, t, :],
                     func=FUNC.Square,
-                    bias=shift[i][:, t : t + 1],
-                    scale=1.0,
+                    bias=sum_of[i][:, t : t + 1],
+                    scale=-1.0 * D_OUT,
                     accum_out=square_sums[:, t : t + 1],
                 )
-            deviation = norm_pool.tile([P, GROUP], F32)
+            inverse = norm_pool.tile([P, slots], F32, tag="inverse")
             nc.scalar.activation(
-                out=deviation[:], in_=square_sums[:], func=FUNC.Sqrt, bias=eps[:, 0:1], scale=1.0 / D_OUT
+                out=inverse[:],
+                in_=square_sums[:],
+                func=FUNC.Abs_reciprocal_sqrt,
+                bias=eps[:, 0:1],
+                scale=1.0 / D_OUT**3,
             )
-            std[i] = deviation
-
-        def invert(i):
-            inverse = norm_pool.tile([P, GROUP], F32)
-            nc.vector.reciprocal(out=inverse[:], in_=std[i][:])
             inverse_of[i] = inverse
 
         def finish(i):
-            result = norm_pool.tile([P, GROUP, D_OUT], F32)
-            for t in range(GROUP):
+            slots = DUO * GROUP_DUOS[i]
+            result = norm_pool.tile([P, slots, D_OUT], F32, tag="result")
+            for t in range(slots):
                 nc.vector.scalar_tensor_tensor(
                     out=result[:, t, :],
                     in0=centred[i][:, t, :],
@@ -216,11 +226,11 @@ def tile_multiheadattention_pb_t_kernel(
                     op0=MULT,
                     op1=ADD,
                 )
-            nc.sync.dma_start(out=out_by_slot[:, GROUP * i : GROUP * (i + 1), :], in_=result[:])
+            nc.sync.dma_start(out=out_by_slot[:, FIRST_SLOT[i] : FIRST_SLOT[i] + slots, :], in_=result[:])
 
-        def run(stage, i, *args):
+        def run(stage, i):
             if 0 <= i < N_GROUPS:
-                stage(i, *args)
+                stage(i)
 
         def repeat_vectors():
             nc.tensor.matmul(out=repeated[:], lhsT=ones[:], rhs=vector_rows[:], start=True, stop=True)
@@ -245,17 +255,16 @@ def tile_multiheadattention_pb_t_kernel(
                 nc.sync.dma_start(out=vector_rows[0:1, row, :], in_=vector.rearrange("(o d) -> o d", o=1))
             for i in range(1, LOADS_AHEAD):
                 load(i)
-            for step in range(N_GROUPS + 5):
+            for step in range(N_GROUPS + 3):
                 run(load, step + LOADS_AHEAD)
-                run(spread, step - 3)
+                run(quantise, step - 1)
+                run(add_residual, step - 2)
+                run(mean, step - 2)
                 run(turn, step)
                 if step == 0:
                     repeat_vectors()
+                run(spread, step - 2)
                 run(add_bias, step)
-                run(quantise, step - 1)
                 run(multiply, step - 1)
-                run(centre, step - 3)
-                run(add_residual, step - 2)
-                run(finish, step - 5)
-                run(mean, step - 2)
-                run(invert, step - 4)
+                run(finish, step - 3)
+                run(centre, step - 2)

@@ -115,16 +115,20 @@ def tile_multiheadattention_pb_t_kernel(
                     )
             x_grouped[i] = grouped
 
-        def add_bias(i):
-            slots = DUO * GROUP_DUOS[i]
-            biased = norm_pool.tile([P, slots, D_OUT], F32, tag="biased")
+        def add_bias(i, half):
+            slots = GROUP_DUOS[i]
+            if half == 0:
+                r_biased[i] = norm_pool.tile([P, DUO * slots, D_OUT], F32, tag="biased", name="biased")
             nc.gpsimd.tensor_tensor(
-                out=biased[:],
-                in0=r_raw[i][:],
+                out=r_biased[i][:, slots * half : slots * (half + 1), :],
+                in0=r_raw[i][:, slots * half : slots * (half + 1), :],
                 in1=bias_rows.unsqueeze(1).to_broadcast([P, slots, D_OUT]),
                 op=ADD,
             )
-            r_biased[i] = biased
+
+        def wait_for_codes(i):
+            seen = norm_pool.tile([P, 1], U32, tag="seen")
+            nc.gpsimd.tensor_copy(out=seen[:], in_=x_codes[i][:, 0, 0, 0:1])
 
         def quantise(i):
             duos = GROUP_DUOS[i]
@@ -238,6 +242,9 @@ def tile_multiheadattention_pb_t_kernel(
 
         with tc.manual_schedule():
             load(0)
+            for row, vector in enumerate([proj_b, ln_g, ln_b]):
+                nc.sync.dma_start(out=vector_rows[0:1, row, :], in_=vector.rearrange("(o d) -> o d", o=1))
+            load(1)
             words_by_duo = proj_w_words.rearrange("g (a h q) b -> h q (g a) b", h=DUO, q=QUADS)
             scales_by_duo = proj_w_scales.rearrange("g (a h r) n -> h r (g a) n", h=DUO, r=QUADS // 8)
             for h in range(DUO):
@@ -251,20 +258,24 @@ def tile_multiheadattention_pb_t_kernel(
                         out=w_scales[quarter : quarter + QUADS // 8, :, t, :].bitcast(I32),
                         in_=scales_by_duo[h].bitcast(I32),
                     )
-            for row, vector in enumerate([proj_b, ln_g, ln_b]):
-                nc.sync.dma_start(out=vector_rows[0:1, row, :], in_=vector.rearrange("(o d) -> o d", o=1))
-            for i in range(1, LOADS_AHEAD):
+            for i in range(2, LOADS_AHEAD):
                 load(i)
             for step in range(N_GROUPS + 3):
                 run(load, step + LOADS_AHEAD)
                 run(quantise, step - 1)
                 run(add_residual, step - 2)
-                run(mean, step - 2)
                 run(turn, step)
-                if step == 0:
+                if step == 1:
                     repeat_vectors()
+                    add_bias(0, 0)
+                    add_bias(0, 1)
+                run(wait_for_codes, step - 1)
+                if 0 < step < N_GROUPS:
+                    add_bias(step, 0)
+                run(mean, step - 2)
+                if 0 < step < N_GROUPS:
+                    add_bias(step, 1)
                 run(spread, step - 2)
-                run(add_bias, step)
                 run(multiply, step - 1)
                 run(finish, step - 3)
                 run(centre, step - 2)

@@ -82,15 +82,20 @@ def tile_multiheadattention_pb_t_kernel(
         r_biased = {}
         centred = {}
 
+        def load_duo(i, s):
+            if s == 0:
+                x_raw[i] = x_pool.tile([P, GROUP_DUOS[i], HEADS, DUO, HEAD_DIM], BF16, tag="raw", name="raw")
+            first = FIRST_SLOT[i] + DUO * s
+            cuts = [0, 2, HEADS] if i == 0 and s == 0 else [0, HEADS]
+            for a, b in zip(cuts[:-1], cuts[1:]):
+                nc.sync.dma_start(out=x_raw[i][:, s, a:b], in_=x_by_slot[:, a:b, first : first + DUO, :])
+
         def load(i):
+            for s in range(GROUP_DUOS[i]):
+                load_duo(i, s)
+
+        def load_rest(i):
             duos = GROUP_DUOS[i]
-            raw = x_pool.tile([P, duos, HEADS, DUO, HEAD_DIM], BF16, tag="raw")
-            cuts = [0, 2, 4, HEADS] if i == 0 else [0, HEADS]
-            for s in range(duos):
-                first = FIRST_SLOT[i] + DUO * s
-                for a, b in zip(cuts[:-1], cuts[1:]):
-                    nc.sync.dma_start(out=raw[:, s, a:b], in_=x_by_slot[:, a:b, first : first + DUO, :])
-            x_raw[i] = raw
             rest = x_pool.tile([P, DUO * duos, D_OUT], BF16, tag="rest")
             nc.sync.dma_start(out=rest[:], in_=r_by_slot[:, FIRST_SLOT[i] : FIRST_SLOT[i] + DUO * duos, :])
             r_raw[i] = rest
@@ -241,13 +246,10 @@ def tile_multiheadattention_pb_t_kernel(
             nc.vector.tensor_copy(out=bias_copy[:], in_=repeated[:, 0, :])
 
         with tc.manual_schedule():
-            load(0)
-            for row, vector in enumerate([proj_b, ln_g, ln_b]):
-                nc.sync.dma_start(out=vector_rows[0:1, row, :], in_=vector.rearrange("(o d) -> o d", o=1))
-            load(1)
             words_by_duo = proj_w_words.rearrange("g (a h q) b -> h q (g a) b", h=DUO, q=QUADS)
             scales_by_duo = proj_w_scales.rearrange("g (a h r) n -> h r (g a) n", h=DUO, r=QUADS // 8)
-            for h in range(DUO):
+
+            def load_weights(h):
                 for t in range(DUO):
                     quarter = QUADS * (DUO * h + t)
                     nc.sync.dma_start(
@@ -258,10 +260,24 @@ def tile_multiheadattention_pb_t_kernel(
                         out=w_scales[quarter : quarter + QUADS // 8, :, t, :].bitcast(I32),
                         in_=scales_by_duo[h].bitcast(I32),
                     )
+
+            for row, vector in enumerate([proj_b, ln_g, ln_b]):
+                nc.gpsimd.dma_start(out=vector_rows[0:1, row, :], in_=vector.rearrange("(o d) -> o d", o=1))
+            load(0)
+            load_duo(1, 0)
+            load_weights(0)
+            load_duo(1, 1)
+            load_weights(1)
+            load_rest(0)
+            load_rest(1)
+            load(2)
             for i in range(2, LOADS_AHEAD):
-                load(i)
+                if i > 2:
+                    load(i)
+                load_rest(i)
             for step in range(N_GROUPS + 3):
                 run(load, step + LOADS_AHEAD)
+                run(load_rest, step + LOADS_AHEAD)
                 run(quantise, step - 1)
                 run(add_residual, step - 2)
                 run(turn, step)
@@ -269,11 +285,15 @@ def tile_multiheadattention_pb_t_kernel(
                     repeat_vectors()
                     add_bias(0, 0)
                     add_bias(0, 1)
-                run(wait_for_codes, step - 1)
-                if 0 < step < N_GROUPS:
+                if step > 2:
+                    run(wait_for_codes, step - 1)
+                if 2 < step < N_GROUPS:
                     add_bias(step, 0)
                 run(mean, step - 2)
-                if 0 < step < N_GROUPS:
+                if 2 < step < N_GROUPS:
+                    add_bias(step, 1)
+                if 0 < step < 3:
+                    add_bias(step, 0)
                     add_bias(step, 1)
                 run(spread, step - 2)
                 run(multiply, step - 1)

@@ -51,6 +51,8 @@ def tile_multiheadattention_pb_t_kernel(
         rows_psum = stack.enter_context(tc.psum_pool(name="rows", bufs=1))
         acc_psum = stack.enter_context(tc.psum_pool(name="acc", bufs=2))
 
+        vector_rows = const.tile([P, ROWS, D_OUT], BF16)
+        nc.vector.memset(vector_rows[:], 0.0)
         w_words = const.tile([P, HEAD_DUOS, DUO, 2 * D_OUT], U8, align_bytes=64)
         nc.vector.memset(w_words[:].bitcast(I32), 0)
         w_scales = const.tile([P, HEAD_DUOS, DUO, D_OUT], U8, align_bytes=64)
@@ -59,8 +61,6 @@ def tile_multiheadattention_pb_t_kernel(
         make_identity(nc, identity[:])
         eps = const.tile([P, 1], F32)
         nc.vector.memset(eps[:], LN_EPS)
-        vector_rows = const.tile([P, ROWS, D_OUT], BF16)
-        nc.vector.memset(vector_rows[:], 0.0)
         ones = const.tile([P, P], BF16)
         nc.vector.memset(ones[:], 1.0)
         repeated = rows_psum.tile([P, ROWS, D_OUT], F32)
@@ -86,7 +86,7 @@ def tile_multiheadattention_pb_t_kernel(
             if s == 0:
                 x_raw[i] = x_pool.tile([P, GROUP_DUOS[i], HEADS, DUO, HEAD_DIM], BF16, tag="raw", name="raw")
             first = FIRST_SLOT[i] + DUO * s
-            cuts = [0, 2, HEADS] if i == 0 and s == 0 else [0, HEADS]
+            cuts = [0, 4, HEADS] if i == 0 and s == 0 else [0, HEADS]
             for a, b in zip(cuts[:-1], cuts[1:]):
                 nc.sync.dma_start(out=x_raw[i][:, s, a:b], in_=x_by_slot[:, a:b, first : first + DUO, :])
 
@@ -261,14 +261,15 @@ def tile_multiheadattention_pb_t_kernel(
                         in_=scales_by_duo[h].bitcast(I32),
                     )
 
+            load_duo(0, 0)
             for row, vector in enumerate([proj_b, ln_g, ln_b]):
-                nc.gpsimd.dma_start(out=vector_rows[0:1, row, :], in_=vector.rearrange("(o d) -> o d", o=1))
-            load(0)
+                nc.sync.dma_start(out=vector_rows[0:1, row, :], in_=vector.rearrange("(o d) -> o d", o=1))
+            load_duo(0, 1)
             load_duo(1, 0)
             load_weights(0)
             load_duo(1, 1)
-            load_weights(1)
             load_rest(0)
+            load_weights(1)
             load_rest(1)
             load(2)
             for i in range(2, LOADS_AHEAD):
@@ -292,9 +293,10 @@ def tile_multiheadattention_pb_t_kernel(
                 run(mean, step - 2)
                 if 2 < step < N_GROUPS:
                     add_bias(step, 1)
-                if 0 < step < 3:
-                    add_bias(step, 0)
-                    add_bias(step, 1)
+                if step == 2:
+                    for i in (1, 2):
+                        add_bias(i, 0)
+                        add_bias(i, 1)
                 run(spread, step - 2)
                 run(multiply, step - 1)
                 run(finish, step - 3)

@@ -29,7 +29,7 @@ ROWS = 4
 GROUP_DUOS = [2] * 15 + [1, 1]
 N_GROUPS = len(GROUP_DUOS)
 FIRST_SLOT = [DUO * sum(GROUP_DUOS[:i]) for i in range(N_GROUPS)]
-LOADS_AHEAD = 6
+LOADS_AHEAD = 10
 
 FLOPS = 2 * TOKENS * HEADS * HEAD_DIM * D_OUT
 
@@ -47,6 +47,7 @@ def tile_multiheadattention_pb_t_kernel(
         x_pool = stack.enter_context(tc.tile_pool(name="x", bufs=LOADS_AHEAD + 2))
         quant_pool = stack.enter_context(tc.tile_pool(name="quant", bufs=3))
         norm_pool = stack.enter_context(tc.tile_pool(name="norm", bufs=5))
+        result_pool = stack.enter_context(tc.tile_pool(name="result", bufs=13))
         turned_psum = stack.enter_context(tc.psum_pool(name="turned", bufs=5))
         rows_psum = stack.enter_context(tc.psum_pool(name="rows", bufs=1))
         acc_psum = stack.enter_context(tc.psum_pool(name="acc", bufs=2))
@@ -225,7 +226,7 @@ def tile_multiheadattention_pb_t_kernel(
 
         def finish(i):
             slots = DUO * GROUP_DUOS[i]
-            result = norm_pool.tile([P, slots, D_OUT], F32, tag="result")
+            result = result_pool.tile([P, slots, D_OUT], F32, tag="result")
             for t in range(slots):
                 nc.vector.scalar_tensor_tensor(
                     out=result[:, t, :],

@@ -81,6 +81,7 @@ def tile_multiheadattention_pb_t_kernel(
         inverse_of = {}
         acc = {}
         r_biased = {}
+        square_sums_of = {}
         centred = {}
 
         def load_duo(i, s):
@@ -107,6 +108,8 @@ def tile_multiheadattention_pb_t_kernel(
             span = DUO * DUO * PAIRS
             grouped = quant_pool.tile([P, duos, HEAD_DUOS, P, 4], BF16, align_bytes=64, tag="grouped")
             for s in range(duos):
+                if s == duos - 1:
+                    run(invert, i - 3)
                 for half in range(HEAD_DUOS // 2):
                     turned = turned_psum.tile([P, 2, 2, P], F32, tag="turned")
                     for k in range(2):
@@ -203,21 +206,24 @@ def tile_multiheadattention_pb_t_kernel(
 
         def spread(i):
             slots = DUO * GROUP_DUOS[i]
-            squares = norm_pool.tile([P, D_OUT], F32, tag="squares")
+            squares = norm_pool.tile([P, slots, D_OUT], F32, tag="squares")
             square_sums = norm_pool.tile([P, slots], F32, tag="square_sums")
             for t in range(slots):
                 nc.scalar.activation(
-                    out=squares[:],
+                    out=squares[:, t, :],
                     in_=summed[i][:, t, :],
                     func=FUNC.Square,
                     bias=sum_of[i][:, t : t + 1],
                     scale=-1.0 * D_OUT,
                     accum_out=square_sums[:, t : t + 1],
                 )
-            inverse = norm_pool.tile([P, slots], F32, tag="inverse")
+            square_sums_of[i] = square_sums
+
+        def invert(i):
+            inverse = norm_pool.tile([P, DUO * GROUP_DUOS[i]], F32, tag="inverse")
             nc.scalar.activation(
                 out=inverse[:],
-                in_=square_sums[:],
+                in_=square_sums_of[i][:],
                 func=FUNC.Abs_reciprocal_sqrt,
                 bias=eps[:, 0:1],
                 scale=1.0 / D_OUT**3,
@@ -299,6 +305,8 @@ def tile_multiheadattention_pb_t_kernel(
                         add_bias(i, 0)
                         add_bias(i, 1)
                 run(spread, step - 2)
+                if step >= N_GROUPS - 1:
+                    run(invert, step - 2)
                 run(multiply, step - 1)
                 run(finish, step - 3)
                 run(centre, step - 2)

from contextlib import ExitStack

import concourse.mybir as mybir
from concourse.masks import make_identity

F32 = mybir.dt.float32
BF16 = mybir.dt.bfloat16
I32 = mybir.dt.int32
U32 = mybir.dt.uint32
U8 = mybir.dt.uint8
FP8X4 = mybir.dt.float8_e4m3fn_x4
FP4X4 = mybir.dt.float4_e2m1fn_x4
ADD = mybir.AluOpType.add
MULT = mybir.AluOpType.mult
FUNC = mybir.ActivationFunctionType

P = 128
TOKENS = 8192
HEADS = 8
HEAD_DIM = 128
D_OUT = 128
LN_EPS = 1e-5
SLOTS = TOKENS // P
PAIRS = HEAD_DIM // 2
QUADS = HEAD_DIM // 4
DUO = 2
HEAD_DUOS = HEADS // DUO
ROWS = 4
GROUP_DUOS = [2] * 15 + [1, 1]
N_GROUPS = len(GROUP_DUOS)
FIRST_SLOT = [DUO * sum(GROUP_DUOS[:i]) for i in range(N_GROUPS)]
LOADS_AHEAD = 10

FLOPS = 2 * TOKENS * HEADS * HEAD_DIM * D_OUT


def tile_multiheadattention_pb_t_kernel(
    tc, attn_out, residual, proj_w_words, proj_w_scales, proj_b, ln_g, ln_b, out
):
    nc = tc.nc
    x_by_slot = attn_out.rearrange("h (p t) j -> p h t j", p=P)
    r_by_slot = residual.rearrange("(p t) d -> p t d", p=P)
    out_by_slot = out.rearrange("(p t) d -> p t d", p=P)

    with ExitStack() as stack:
        const = stack.enter_context(tc.tile_pool(name="const", bufs=1))
        x_pool = stack.enter_context(tc.tile_pool(name="x", bufs=LOADS_AHEAD + 2))
        quant_pool = stack.enter_context(tc.tile_pool(name="quant", bufs=3))
        norm_pool = stack.enter_context(tc.tile_pool(name="norm", bufs=5))
        result_pool = stack.enter_context(tc.tile_pool(name="result", bufs=13))
        turned_psum = stack.enter_context(tc.psum_pool(name="turned", bufs=5))
        rows_psum = stack.enter_context(tc.psum_pool(name="rows", bufs=1))
        acc_psum = stack.enter_context(tc.psum_pool(name="acc", bufs=2))

        vector_rows = const.tile([P, ROWS, D_OUT], BF16)
        nc.vector.memset(vector_rows[:], 0.0)
        w_words = const.tile([P, HEAD_DUOS, DUO, 2 * D_OUT], U8, align_bytes=64)
        nc.vector.memset(w_words[:].bitcast(I32), 0)
        w_scales = const.tile([P, HEAD_DUOS, DUO, D_OUT], U8, align_bytes=64)
        nc.vector.memset(w_scales[:].bitcast(I32), 0)
        identity = const.tile([P, P], F32)
        make_identity(nc, identity[:])
        eps = const.tile([P, 1], F32)
        nc.vector.memset(eps[:], LN_EPS)
        ones = const.tile([P, P], BF16)
        nc.vector.memset(ones[:], 1.0)
        repeated = rows_psum.tile([P, ROWS, D_OUT], F32)
        bias_copy = const.tile([P, D_OUT], F32)
        bias_rows = bias_copy[:]
        gain_rows = repeated[:, 1, :]
        shift_rows = repeated[:, 2, :]

        x_raw = {}
        r_raw = {}
        x_grouped = {}
        x_codes = {}
        x_scales = {}
        summed = {}
        sum_of = {}
        shift = {}
        inverse_of = {}
        acc = {}
        r_biased = {}
        square_sums_of = {}
        centred = {}

        def load_duo(i, s):
            if s == 0:
                x_raw[i] = x_pool.tile([P, GROUP_DUOS[i], HEADS, DUO, HEAD_DIM], BF16, tag="raw", name="raw")
            first = FIRST_SLOT[i] + DUO * s
            cuts = [0, 4, HEADS] if i == 0 and s == 0 else [0, HEADS]
            for a, b in zip(cuts[:-1], cuts[1:]):
                nc.sync.dma_start(out=x_raw[i][:, s, a:b], in_=x_by_slot[:, a:b, first : first + DUO, :])

        def load(i):
            for s in range(GROUP_DUOS[i]):
                load_duo(i, s)

        def load_rest(i):
            duos = GROUP_DUOS[i]
            rest = x_pool.tile([P, DUO * duos, D_OUT], BF16, tag="rest")
            nc.sync.dma_start(out=rest[:], in_=r_by_slot[:, FIRST_SLOT[i] : FIRST_SLOT[i] + DUO * duos, :])
            r_raw[i] = rest

        def turn(i):
            duos = GROUP_DUOS[i]
            words = x_raw[i][:].bitcast(F32).rearrange("p s h t w -> p s (h t w)")
            span = DUO * DUO * PAIRS
            grouped = quant_pool.tile([P, duos, HEAD_DUOS, P, 4], BF16, align_bytes=64, tag="grouped")
            for s in range(duos):
                if s == duos - 1:
                    run(invert, i - 3)
                for half in range(HEAD_DUOS // 2):
                    turned = turned_psum.tile([P, 2, 2, P], F32, tag="turned")
                    for k in range(2):
                        d = 2 * half + k
                        for u in range(2):
                            nc.tensor.transpose(
                                turned[:, k, u, :], words[:, s, span * d + u : span * (d + 1) : 2], identity[:]
                            )
                    nc.scalar.copy(
                        out=grouped[:, s, 2 * half : 2 * half + 2].bitcast(F32),
                        in_=turned[:].rearrange("p k u m -> p k m u"),
                    )
            x_grouped[i] = grouped

        def add_bias(i, half):
            slots = GROUP_DUOS[i]
            if half == 0:
                r_biased[i] = norm_pool.tile([P, DUO * slots, D_OUT], F32, tag="biased", name="biased")
            nc.gpsimd.tensor_tensor(
                out=r_biased[i][:, slots * half : slots * (half + 1), :],
                in0=r_raw[i][:, slots * half : slots * (half + 1), :],
                in1=bias_rows.unsqueeze(1).to_broadcast([P, slots, D_OUT]),
                op=ADD,
            )

        def wait_for_codes(i):
            seen = norm_pool.tile([P, 1], U32, tag="seen")
            nc.gpsimd.tensor_copy(out=seen[:], in_=x_codes[i][:, 0, 0, 0:1])

        def quantise(i):
            duos = GROUP_DUOS[i]
            codes = quant_pool.tile([P, duos, HEAD_DUOS, P], U32, align_bytes=64, tag="codes")
            scales = quant_pool.tile([P, duos, HEAD_DUOS, P], U8, align_bytes=64, tag="scales")
            nc.vector.quantize_mx(
                out=codes[:].rearrange("p s d m -> p (s d m)").bitcast(FP8X4),
                scales=scales[:].rearrange("p s d m -> p (s d m)"),
                in_=x_grouped[i][:].rearrange("p s d m k -> p (s d m k)"),
            )
            x_codes[i] = codes
            x_scales[i] = scales

        def multiply(i):
            duos = GROUP_DUOS[i]
            products = acc_psum.tile([P, DUO * duos, D_OUT], F32, tag="products")
            for s in range(duos):
                for t in range(DUO):
                    for d in range(HEAD_DUOS):
                        nc.tensor.matmul_mx(
                            out=products[:, DUO * s + t, :],
                            lhsT=x_codes[i][:, s, d, :].bitcast(FP8X4),
                            lhsT_scale=x_scales[i][:, s, d, :],
                            rhs=w_words[:, d, t, :].bitcast(FP4X4),
                            rhs_scale=w_scales[:, d, t, :],
                            start=(d == 0),
                            stop=(d == HEAD_DUOS - 1),
                        )
            acc[i] = products

        def add_residual(i):
            slots = DUO * GROUP_DUOS[i]
            y = norm_pool.tile([P, slots, D_OUT], F32, tag="y")
            sums = norm_pool.tile([P, slots], F32, tag="sums")
            for t in range(slots):
                nc.vector.scalar_tensor_tensor(
                    out=y[:, t, :],
                    in0=acc[i][:, t, :],
                    scalar=1.0,
                    in1=r_biased[i][:, t, :],
                    op0=MULT,
                    op1=ADD,
                    accum_out=sums[:, t : t + 1],
                )
            summed[i] = y
            sum_of[i] = sums

        def mean(i):
            minus_mean = norm_pool.tile([P, DUO * GROUP_DUOS[i]], F32, tag="minus_mean")
            nc.gpsimd.tensor_scalar_mul(out=minus_mean[:], in0=sum_of[i][:], scalar1=-1.0 / D_OUT)
            shift[i] = minus_mean

        def centre(i):
            slots = DUO * GROUP_DUOS[i]
            gained = norm_pool.tile([P, slots, D_OUT], F32, tag="gained")
            for t in range(slots):
                nc.vector.scalar_tensor_tensor(
                    out=gained[:, t, :],
                    in0=summed[i][:, t, :],
                    scalar=shift[i][:, t : t + 1],
                    in1=gain_rows,
                    op0=ADD,
                    op1=MULT,
                )
            centred[i] = gained

        def spread(i):
            slots = DUO * GROUP_DUOS[i]
            squares = norm_pool.tile([P, slots, D_OUT], F32, tag="squares")
            square_sums = norm_pool.tile([P, slots], F32, tag="square_sums")
            for t in range(slots):
                nc.scalar.activation(
                    out=squares[:, t, :],
                    in_=summed[i][:, t, :],
                    func=FUNC.Square,
                    bias=sum_of[i][:, t : t + 1],
                    scale=-1.0 * D_OUT,
                    accum_out=square_sums[:, t : t + 1],
                )
            square_sums_of[i] = square_sums

        def invert(i):
            inverse = norm_pool.tile([P, DUO * GROUP_DUOS[i]], F32, tag="inverse")
            nc.scalar.activation(
                out=inverse[:],
                in_=square_sums_of[i][:],
                func=FUNC.Abs_reciprocal_sqrt,
                bias=eps[:, 0:1],
                scale=1.0 / D_OUT**3,
            )
            inverse_of[i] = inverse

        def finish(i):
            slots = DUO * GROUP_DUOS[i]
            result = result_pool.tile([P, slots, D_OUT], F32, tag="result")
            for t in range(slots):
                nc.vector.scalar_tensor_tensor(
                    out=result[:, t, :],
                    in0=centred[i][:, t, :],
                    scalar=inverse_of[i][:, t : t + 1],
                    in1=shift_rows,
                    op0=MULT,
                    op1=ADD,
                )
            nc.sync.dma_start(out=out_by_slot[:, FIRST_SLOT[i] : FIRST_SLOT[i] + slots, :], in_=result[:])

        def run(stage, i):
            if 0 <= i < N_GROUPS:
                stage(i)

        def repeat_vectors():
            nc.tensor.matmul(out=repeated[:], lhsT=ones[:], rhs=vector_rows[:], start=True, stop=True)
            nc.vector.tensor_copy(out=bias_copy[:], in_=repeated[:, 0, :])

        with tc.manual_schedule():
            words_by_duo = proj_w_words.rearrange("g (a h q) b -> h q (g a) b", h=DUO, q=QUADS)
            scales_by_duo = proj_w_scales.rearrange("g (a h r) n -> h r (g a) n", h=DUO, r=QUADS // 8)

            def load_weights(h):
                for t in range(DUO):
                    quarter = QUADS * (DUO * h + t)
                    nc.sync.dma_start(
                        out=w_words[quarter : quarter + QUADS, :, t, :].bitcast(I32),
                        in_=words_by_duo[h].bitcast(I32),
                    )
                    nc.sync.dma_start(
                        out=w_scales[quarter : quarter + QUADS // 8, :, t, :].bitcast(I32),
                        in_=scales_by_duo[h].bitcast(I32),
                    )

            load_duo(0, 0)
            for row, vector in enumerate([proj_b, ln_g, ln_b]):
                nc.sync.dma_start(out=vector_rows[0:1, row, :], in_=vector.rearrange("(o d) -> o d", o=1))
            load_duo(0, 1)
            load_duo(1, 0)
            load_weights(0)
            load_duo(1, 1)
            load_rest(0)
            load_weights(1)
            load_rest(1)
            load(2)
            for i in range(2, LOADS_AHEAD):
                if i > 2:
                    load(i)
                load_rest(i)
            for step in range(N_GROUPS + 3):
                run(load, step + LOADS_AHEAD)
                run(load_rest, step + LOADS_AHEAD)
                run(quantise, step - 1)
                run(add_residual, step - 2)
                run(turn, step)
                if step == 1:
                    repeat_vectors()
                    add_bias(0, 0)
                    add_bias(0, 1)
                if step > 2:
                    run(wait_for_codes, step - 1)
                if 2 < step < N_GROUPS:
                    add_bias(step, 0)
                run(mean, step - 2)
                if 2 < step < N_GROUPS:
                    add_bias(step, 1)
                if step == 2:
                    for i in (1, 2):
                        add_bias(i, 0)
                        add_bias(i, 1)
                run(spread, step - 2)
                if step >= N_GROUPS - 1:
                    run(invert, step - 2)
                run(multiply, step - 1)
                run(finish, step - 3)
                run(centre, step - 2)
